import numpy as np
import ml_dtypes

BF16 = ml_dtypes.bfloat16


def bf(x):
    return np.asarray(x, np.float32).astype(BF16)


def f32(x):
    return np.asarray(x, np.float32)


def f64(x):
    return np.asarray(x).astype(np.float64)


def striped(idx):
    return np.tile(idx.reshape(-1, 16).T, (8, 1))


E, C, S, K, M, N = 4, 128, 512, 512, 512, 2048


def setup_inputs():
    x = f32(np.random.standard_normal((E, C, S)))
    gate = f32(np.tile(0.5 + np.random.rand(N)[None, :], (C, 1)))
    w = bf(np.random.standard_normal((E, C, M)) / np.sqrt(C))
    bias = f32(0.1 * np.random.standard_normal((M, 1)))
    return {"x": x, "gate": gate, "w": w, "bias": bias, "offs": striped(np.concatenate([np.random.permutation(S) for _ in range(-(-(N) // S))])[:N])}


def reference(x, gate, w, bias, offs):
    idx = offs[:16].T.reshape(-1)
    x, gate, w, bias = f64(x), f64(gate), f64(w), f64(bias)
    cols = []
    for e in range(E):
        sl = slice(e * K, (e + 1) * K)
        xd = x[e][:, idx[sl]] * gate[:, sl]
        cols.append(w[e].T @ xd + bias)
    return np.concatenate(cols, axis=1)

@@ -1,0 +1,66 @@
+import concourse.mybir as mybir
+from concourse.masks import make_identity
+
+E, C, S, K, M, N = 4, 128, 512, 512, 512, 2048
+P = 128
+MB = M // P
+COLS = K // 16
+F32, BF16, U16 = mybir.dt.float32, mybir.dt.bfloat16, mybir.dt.uint16
+MULT = mybir.AluOpType.mult
+IDENTITY = mybir.ActivationFunctionType.Identity
+
+FLOPS = 2 * C * M * N
+
+
+def tile_expertschoosemaskedexpand_kernel(tc, x, gate, w, bias, offs, out):
+    nc = tc.nc
+    with (
+        tc.tile_pool(name="held", bufs=1) as held,
+        tc.tile_pool(name="slots", bufs=2) as slots,
+        tc.tile_pool(name="results", bufs=8) as results,
+        tc.psum_pool(name="banks", bufs=6) as banks,
+        tc.psum_pool(name="bias_bank", bufs=1) as bias_bank,
+    ):
+        offsets = held.tile([P, N // 16], U16, name="offsets")
+        nc.sync.dma_start(offsets[:], offs)
+        bias_rows = held.tile([MB, P], F32, name="bias_rows")
+        nc.scalar.dma_start(bias_rows[:], bias.rearrange("(b p) o -> b (p o)", p=P))
+        tables, gates, weights = [], [], []
+        for e in range(E):
+            table = held.tile([C, S], F32, name=f"table{e}")
+            nc.sync.dma_start(table[:], x[e])
+            gate_e = held.tile([C, K], F32, name=f"gate{e}")
+            nc.scalar.dma_start(gate_e[:], gate[:, e * K : (e + 1) * K])
+            weight = held.tile([C, M], BF16, name=f"weight{e}")
+            nc.scalar.dma_start(weight[:], w[e])
+            tables.append(table)
+            gates.append(gate_e)
+            weights.append(weight)
+
+        ident = held.tile([MB, MB], F32, name="ident")
+        make_identity(nc, ident[:])
+        bias_psum = bias_bank.tile([P, MB], F32, name="bias_psum")
+        nc.tensor.matmul(bias_psum[:], bias_rows[:], ident[:], start=True, stop=True)
+        bias_cols = held.tile([P, MB], F32, name="bias_cols")
+        nc.vector.tensor_copy(bias_cols[:], bias_psum[:])
+
+        for e in range(E):
+            product = slots.tile([C, K], F32, name="product")
+            nc.vector.tensor_tensor(
+                product[:],
+                tables[e][:].indirect(offsets[:, e * COLS : (e + 1) * COLS]),
+                gates[e][:],
+                MULT,
+            )
+            rounded = slots.tile([C, K], BF16, name="rounded")
+            nc.vector.tensor_copy(rounded[:], product[:])
+
+            for b in range(MB):
+                bank = banks.tile([P, K], F32, name="bank")
+                nc.tensor.matmul(bank[:], weights[e][:, b * P : (b + 1) * P], rounded[:], start=True, stop=True)
+                result = results.tile([P, K], F32, name="result")
+                if b == MB - 1:
+                    nc.vector.tensor_scalar_add(result[:], bank[:], bias_cols[:, b : b + 1])
+                else:
+                    nc.scalar.activation(result[:], bank[:], IDENTITY, bias=bias_cols[:, b : b + 1])
+                nc.sync.dma_start(out[b * P : (b + 1) * P, e * K : (e + 1) * K], result[:])

@@ -1,5 +1,4 @@
 import concourse.mybir as mybir
-from concourse.masks import make_identity
 
 E, C, S, K, M, N = 4, 128, 512, 512, 512, 2048
 P = 128
@@ -14,17 +13,17 @@ FLOPS = 2 * C * M * N
 
 def tile_expertschoosemaskedexpand_kernel(tc, x, gate, w, bias, offs, out):
     nc = tc.nc
+    out_groups = out.rearrange("(p b) n -> p b n", b=MB)
     with (
         tc.tile_pool(name="held", bufs=1) as held,
-        tc.tile_pool(name="slots", bufs=2) as slots,
-        tc.tile_pool(name="results", bufs=8) as results,
+        tc.tile_pool(name="slots", bufs=E) as slots,
+        tc.tile_pool(name="results", bufs=E * MB) as results,
         tc.psum_pool(name="banks", bufs=6) as banks,
-        tc.psum_pool(name="bias_bank", bufs=1) as bias_bank,
     ):
         offsets = held.tile([P, N // 16], U16, name="offsets")
         nc.sync.dma_start(offsets[:], offs)
-        bias_rows = held.tile([MB, P], F32, name="bias_rows")
-        nc.scalar.dma_start(bias_rows[:], bias.rearrange("(b p) o -> b (p o)", p=P))
+        bias_cols = held.tile([P, MB], F32, name="bias_cols")
+        nc.scalar.dma_start(bias_cols[:], bias.rearrange("(p b) o -> p (b o)", b=MB))
         tables, gates, weights = [], [], []
         for e in range(E):
             table = held.tile([C, S], F32, name=f"table{e}")
@@ -37,14 +36,7 @@ def tile_expertschoosemaskedexpand_kernel(tc, x, gate, w, bias, offs, out):
             gates.append(gate_e)
             weights.append(weight)
 
-        ident = held.tile([MB, MB], F32, name="ident")
-        make_identity(nc, ident[:])
-        bias_psum = bias_bank.tile([P, MB], F32, name="bias_psum")
-        nc.tensor.matmul(bias_psum[:], bias_rows[:], ident[:], start=True, stop=True)
-        bias_cols = held.tile([P, MB], F32, name="bias_cols")
-        nc.vector.tensor_copy(bias_cols[:], bias_psum[:])
-
-        for e in range(E):
+        def look_up(e):
             product = slots.tile([C, K], F32, name="product")
             nc.vector.tensor_tensor(
                 product[:],
@@ -54,13 +46,20 @@ def tile_expertschoosemaskedexpand_kernel(tc, x, gate, w, bias, offs, out):
             )
             rounded = slots.tile([C, K], BF16, name="rounded")
             nc.vector.tensor_copy(rounded[:], product[:])
+            return rounded
 
+        def expand(e, rounded):
+            weight_groups = weights[e][:].rearrange("c (p b) -> c b p", b=MB)
             for b in range(MB):
                 bank = banks.tile([P, K], F32, name="bank")
-                nc.tensor.matmul(bank[:], weights[e][:, b * P : (b + 1) * P], rounded[:], start=True, stop=True)
+                nc.tensor.matmul(bank[:], weight_groups[:, b, :], rounded[:], start=True, stop=True)
                 result = results.tile([P, K], F32, name="result")
-                if b == MB - 1:
+                if e >= E // 2 and b >= MB // 2:
                     nc.vector.tensor_scalar_add(result[:], bank[:], bias_cols[:, b : b + 1])
                 else:
                     nc.scalar.activation(result[:], bank[:], IDENTITY, bias=bias_cols[:, b : b + 1])
-                nc.sync.dma_start(out[b * P : (b + 1) * P, e * K : (e + 1) * K], result[:])
+                nc.sync.dma_start(out_groups[:, b, e * K : (e + 1) * K], result[:])
+
+        rounded_tiles = [look_up(e) for e in range(E)]
+        for e in range(E):
+            expand(e, rounded_tiles[e])

@@ -3,12 +3,13 @@ import concourse.mybir as mybir
 E, C, S, K, M, N = 4, 128, 512, 512, 512, 2048
 P = 128
 MB = M // P
-COLS = K // 16
 F32, BF16, U16 = mybir.dt.float32, mybir.dt.bfloat16, mybir.dt.uint16
 MULT = mybir.AluOpType.mult
 IDENTITY = mybir.ActivationFunctionType.Identity
 
 FLOPS = 2 * C * M * N
+
+PIECES = [(e, 0, K) for e in range(E)]
 
 
 def tile_expertschoosemaskedexpand_kernel(tc, x, gate, w, bias, offs, out):
@@ -16,50 +17,52 @@ def tile_expertschoosemaskedexpand_kernel(tc, x, gate, w, bias, offs, out):
     out_groups = out.rearrange("(p b) n -> p b n", b=MB)
     with (
         tc.tile_pool(name="held", bufs=1) as held,
-        tc.tile_pool(name="slots", bufs=E) as slots,
-        tc.tile_pool(name="results", bufs=E * MB) as results,
+        tc.tile_pool(name="slots", bufs=len(PIECES)) as slots,
+        tc.tile_pool(name="results", bufs=len(PIECES) * MB) as results,
         tc.psum_pool(name="banks", bufs=6) as banks,
     ):
         offsets = held.tile([P, N // 16], U16, name="offsets")
         nc.sync.dma_start(offsets[:], offs)
         bias_cols = held.tile([P, MB], F32, name="bias_cols")
-        nc.scalar.dma_start(bias_cols[:], bias.rearrange("(p b) o -> p (b o)", b=MB))
+        nc.sync.dma_start(bias_cols[:], bias.rearrange("(p b) o -> p (b o)", b=MB))
         tables, gates, weights = [], [], []
         for e in range(E):
             table = held.tile([C, S], F32, name=f"table{e}")
             nc.sync.dma_start(table[:], x[e])
             gate_e = held.tile([C, K], F32, name=f"gate{e}")
-            nc.scalar.dma_start(gate_e[:], gate[:, e * K : (e + 1) * K])
+            nc.sync.dma_start(gate_e[:], gate[:, e * K : (e + 1) * K])
             weight = held.tile([C, M], BF16, name=f"weight{e}")
-            nc.scalar.dma_start(weight[:], w[e])
+            nc.sync.dma_start(weight[:], w[e])
             tables.append(table)
             gates.append(gate_e)
             weights.append(weight)
 
-        def look_up(e):
-            product = slots.tile([C, K], F32, name="product")
+        def look_up(e, first, width):
+            j = e * K + first
+            product = slots.tile([C, width], F32, name="product")
             nc.vector.tensor_tensor(
                 product[:],
-                tables[e][:].indirect(offsets[:, e * COLS : (e + 1) * COLS]),
-                gates[e][:],
+                tables[e][:].indirect(offsets[:, j // 16 : (j + width) // 16]),
+                gates[e][:, first : first + width],
                 MULT,
             )
-            rounded = slots.tile([C, K], BF16, name="rounded")
+            rounded = slots.tile([C, width], BF16, name="rounded")
             nc.vector.tensor_copy(rounded[:], product[:])
             return rounded
 
-        def expand(e, rounded):
+        def expand(e, first, width, rounded):
+            j = e * K + first
             weight_groups = weights[e][:].rearrange("c (p b) -> c b p", b=MB)
             for b in range(MB):
-                bank = banks.tile([P, K], F32, name="bank")
+                bank = banks.tile([P, width], F32, name="bank")
                 nc.tensor.matmul(bank[:], weight_groups[:, b, :], rounded[:], start=True, stop=True)
-                result = results.tile([P, K], F32, name="result")
+                result = results.tile([P, width], F32, name="result")
                 if e >= E // 2 and b >= MB // 2:
                     nc.vector.tensor_scalar_add(result[:], bank[:], bias_cols[:, b : b + 1])
                 else:
                     nc.scalar.activation(result[:], bank[:], IDENTITY, bias=bias_cols[:, b : b + 1])
-                nc.sync.dma_start(out_groups[:, b, e * K : (e + 1) * K], result[:])
+                nc.sync.dma_start(out_groups[:, b, j : j + width], result[:])
 
-        rounded_tiles = [look_up(e) for e in range(E)]
-        for e in range(E):
-            expand(e, rounded_tiles[e])
+        rounded_tiles = [look_up(e, first, width) for e, first, width in PIECES]
+        for (e, first, width), rounded in zip(PIECES, rounded_tiles):
+            expand(e, first, width, rounded)

@@ -3,22 +3,26 @@ import concourse.mybir as mybir
 E, C, S, K, M, N = 4, 128, 512, 512, 512, 2048
 P = 128
 MB = M // P
+COLS = K // 16
 F32, BF16, U16 = mybir.dt.float32, mybir.dt.bfloat16, mybir.dt.uint16
 MULT = mybir.AluOpType.mult
 IDENTITY = mybir.ActivationFunctionType.Identity
 
 FLOPS = 2 * C * M * N
 
-PIECES = [(e, 0, K) for e in range(E)]
+
+def groups_in_a_store(e):
+    return 1 if e == 0 else 2
 
 
 def tile_expertschoosemaskedexpand_kernel(tc, x, gate, w, bias, offs, out):
     nc = tc.nc
     out_groups = out.rearrange("(p b) n -> p b n", b=MB)
+    stores = sum(MB // groups_in_a_store(e) for e in range(E))
     with (
         tc.tile_pool(name="held", bufs=1) as held,
-        tc.tile_pool(name="slots", bufs=len(PIECES)) as slots,
-        tc.tile_pool(name="results", bufs=len(PIECES) * MB) as results,
+        tc.tile_pool(name="slots", bufs=E) as slots,
+        tc.tile_pool(name="results", bufs=stores) as results,
         tc.psum_pool(name="banks", bufs=6) as banks,
     ):
         offsets = held.tile([P, N // 16], U16, name="offsets")
@@ -37,32 +41,32 @@ def tile_expertschoosemaskedexpand_kernel(tc, x, gate, w, bias, offs, out):
             gates.append(gate_e)
             weights.append(weight)
 
-        def look_up(e, first, width):
-            j = e * K + first
-            product = slots.tile([C, width], F32, name="product")
+        def look_up(e):
+            product = slots.tile([C, K], F32, name="product")
             nc.vector.tensor_tensor(
                 product[:],
-                tables[e][:].indirect(offsets[:, j // 16 : (j + width) // 16]),
-                gates[e][:, first : first + width],
+                tables[e][:].indirect(offsets[:, e * COLS : (e + 1) * COLS]),
+                gates[e][:],
                 MULT,
             )
-            rounded = slots.tile([C, width], BF16, name="rounded")
+            rounded = slots.tile([C, K], BF16, name="rounded")
             nc.vector.tensor_copy(rounded[:], product[:])
             return rounded
 
-        def expand(e, first, width, rounded):
-            j = e * K + first
+        def expand(e, rounded):
             weight_groups = weights[e][:].rearrange("c (p b) -> c b p", b=MB)
-            for b in range(MB):
-                bank = banks.tile([P, width], F32, name="bank")
-                nc.tensor.matmul(bank[:], weight_groups[:, b, :], rounded[:], start=True, stop=True)
-                result = results.tile([P, width], F32, name="result")
-                if e >= E // 2 and b >= MB // 2:
-                    nc.vector.tensor_scalar_add(result[:], bank[:], bias_cols[:, b : b + 1])
-                else:
-                    nc.scalar.activation(result[:], bank[:], IDENTITY, bias=bias_cols[:, b : b + 1])
-                nc.sync.dma_start(out_groups[:, b, j : j + width], result[:])
+            span = groups_in_a_store(e)
+            for first in range(0, MB, span):
+                result = results.tile([P, span, K], F32, name="result")
+                for b in range(first, first + span):
+                    bank = banks.tile([P, K], F32, name="bank")
+                    nc.tensor.matmul(bank[:], weight_groups[:, b, :], rounded[:], start=True, stop=True)
+                    if e >= E // 2 and b >= MB // 2:
+                        nc.vector.tensor_scalar_add(result[:, b - first, :], bank[:], bias_cols[:, b : b + 1])
+                    else:
+                        nc.scalar.activation(result[:, b - first, :], bank[:], IDENTITY, bias=bias_cols[:, b : b + 1])
+                nc.sync.dma_start(out_groups[:, first : first + span, e * K : (e + 1) * K], result[:])
 
-        rounded_tiles = [look_up(e, first, width) for e, first, width in PIECES]
-        for (e, first, width), rounded in zip(PIECES, rounded_tiles):
-            expand(e, first, width, rounded)
+        rounded_tiles = [look_up(e) for e in range(E)]
+        for e in range(E):
+            expand(e, rounded_tiles[e])

@@ -11,24 +11,19 @@ IDENTITY = mybir.ActivationFunctionType.Identity
 FLOPS = 2 * C * M * N
 
 
-def groups_in_a_store(e):
-    return 1 if e == 0 else 2
-
-
 def tile_expertschoosemaskedexpand_kernel(tc, x, gate, w, bias, offs, out):
     nc = tc.nc
     out_groups = out.rearrange("(p b) n -> p b n", b=MB)
-    stores = sum(MB // groups_in_a_store(e) for e in range(E))
     with (
         tc.tile_pool(name="held", bufs=1) as held,
         tc.tile_pool(name="slots", bufs=E) as slots,
-        tc.tile_pool(name="results", bufs=stores) as results,
+        tc.tile_pool(name="singles", bufs=2 * MB) as singles,
+        tc.tile_pool(name="doubles", bufs=MB) as doubles,
         tc.psum_pool(name="banks", bufs=6) as banks,
     ):
         offsets = held.tile([P, N // 16], U16, name="offsets")
         nc.sync.dma_start(offsets[:], offs)
         bias_cols = held.tile([P, MB], F32, name="bias_cols")
-        nc.sync.dma_start(bias_cols[:], bias.rearrange("(p b) o -> p (b o)", b=MB))
         tables, gates, weights = [], [], []
         for e in range(E):
             table = held.tile([C, S], F32, name=f"table{e}")
@@ -37,11 +32,14 @@ def tile_expertschoosemaskedexpand_kernel(tc, x, gate, w, bias, offs, out):
             nc.sync.dma_start(gate_e[:], gate[:, e * K : (e + 1) * K])
             weight = held.tile([C, M], BF16, name=f"weight{e}")
             nc.sync.dma_start(weight[:], w[e])
+            if e == 0:
+                nc.sync.dma_start(bias_cols[:], bias.rearrange("(p b) o -> p (b o)", b=MB))
             tables.append(table)
             gates.append(gate_e)
-            weights.append(weight)
+            weights.append(weight[:].rearrange("c (p b) -> c b p", b=MB))
 
-        def look_up(e):
+        rounded = []
+        for e in range(E):
             product = slots.tile([C, K], F32, name="product")
             nc.vector.tensor_tensor(
                 product[:],
@@ -49,24 +47,26 @@ def tile_expertschoosemaskedexpand_kernel(tc, x, gate, w, bias, offs, out):
                 gates[e][:],
                 MULT,
             )
-            rounded = slots.tile([C, K], BF16, name="rounded")
-            nc.vector.tensor_copy(rounded[:], product[:])
-            return rounded
+            rounded_e = slots.tile([C, K], BF16, name="rounded_e")
+            nc.vector.tensor_copy(rounded_e[:], product[:])
+            rounded.append(rounded_e)
 
-        def expand(e, rounded):
-            weight_groups = weights[e][:].rearrange("c (p b) -> c b p", b=MB)
-            span = groups_in_a_store(e)
-            for first in range(0, MB, span):
-                result = results.tile([P, span, K], F32, name="result")
-                for b in range(first, first + span):
-                    bank = banks.tile([P, K], F32, name="bank")
-                    nc.tensor.matmul(bank[:], weight_groups[:, b, :], rounded[:], start=True, stop=True)
-                    if e >= E // 2 and b >= MB // 2:
-                        nc.vector.tensor_scalar_add(result[:, b - first, :], bank[:], bias_cols[:, b : b + 1])
-                    else:
-                        nc.scalar.activation(result[:, b - first, :], bank[:], IDENTITY, bias=bias_cols[:, b : b + 1])
-                nc.sync.dma_start(out_groups[:, first : first + span, e * K : (e + 1) * K], result[:])
+        def expand(e, b):
+            bank = banks.tile([P, K], F32, name="bank")
+            nc.tensor.matmul(bank[:], weights[e][:, b, :], rounded[e][:], start=True, stop=True)
+            return bank
 
-        rounded_tiles = [look_up(e) for e in range(E)]
-        for e in range(E):
-            expand(e, rounded_tiles[e])
+        for e in range(2):
+            for b in range(MB):
+                bank = expand(e, b)
+                single = singles.tile([P, K], F32, name="single")
+                nc.scalar.activation(single[:], bank[:], IDENTITY, bias=bias_cols[:, b : b + 1])
+                nc.sync.dma_start(out_groups[:, b, e * K : (e + 1) * K], single[:])
+
+        for b in range(MB):
+            bank2 = expand(2, b)
+            bank3 = expand(3, b)
+            double = doubles.tile([P, 2 * K], F32, name="double")
+            nc.scalar.activation(double[:, :K], bank2[:], IDENTITY, bias=bias_cols[:, b : b + 1])
+            nc.vector.tensor_scalar_add(double[:, K:], bank3[:], bias_cols[:, b : b + 1])
+            nc.sync.dma_start(out_groups[:, b, 2 * K :], double[:])

@@ -3,10 +3,11 @@ import concourse.mybir as mybir
 E, C, S, K, M, N = 4, 128, 512, 512, 512, 2048
 P = 128
 MB = M // P
-COLS = K // 16
 F32, BF16, U16 = mybir.dt.float32, mybir.dt.bfloat16, mybir.dt.uint16
 MULT = mybir.AluOpType.mult
 IDENTITY = mybir.ActivationFunctionType.Identity
+
+RUNS = [(0, 0, K // 2), (0, K // 2, K // 2)] + [(e, e * K, K) for e in range(1, E)]
 
 FLOPS = 2 * C * M * N
 
@@ -16,57 +17,51 @@ def tile_expertschoosemaskedexpand_kernel(tc, x, gate, w, bias, offs, out):
     out_groups = out.rearrange("(p b) n -> p b n", b=MB)
     with (
         tc.tile_pool(name="held", bufs=1) as held,
-        tc.tile_pool(name="slots", bufs=E) as slots,
-        tc.tile_pool(name="singles", bufs=2 * MB) as singles,
-        tc.tile_pool(name="doubles", bufs=MB) as doubles,
-        tc.psum_pool(name="banks", bufs=6) as banks,
+        tc.tile_pool(name="slots", bufs=len(RUNS)) as slots,
+        tc.tile_pool(name="staged", bufs=len(RUNS) * MB) as staged,
+        tc.psum_pool(name="banks", bufs=8) as banks,
     ):
         offsets = held.tile([P, N // 16], U16, name="offsets")
         nc.sync.dma_start(offsets[:], offs)
         bias_cols = held.tile([P, MB], F32, name="bias_cols")
-        tables, gates, weights = [], [], []
+        tables, weights, gates = {}, {}, {}
         for e in range(E):
             table = held.tile([C, S], F32, name=f"table{e}")
             nc.sync.dma_start(table[:], x[e])
-            gate_e = held.tile([C, K], F32, name=f"gate{e}")
-            nc.sync.dma_start(gate_e[:], gate[:, e * K : (e + 1) * K])
+            tables[e] = table
+            for run in RUNS:
+                if run[0] == e:
+                    gate_run = held.tile([C, run[2]], F32, name=f"gate{run[1]}")
+                    nc.sync.dma_start(gate_run[:], gate[:, run[1] : run[1] + run[2]])
+                    gates[run] = gate_run
             weight = held.tile([C, M], BF16, name=f"weight{e}")
             nc.sync.dma_start(weight[:], w[e])
+            weights[e] = weight[:].rearrange("c (p b) -> c b p", b=MB)
             if e == 0:
                 nc.sync.dma_start(bias_cols[:], bias.rearrange("(p b) o -> p (b o)", b=MB))
-            tables.append(table)
-            gates.append(gate_e)
-            weights.append(weight[:].rearrange("c (p b) -> c b p", b=MB))
 
-        rounded = []
-        for e in range(E):
-            product = slots.tile([C, K], F32, name="product")
+        rounded = {}
+        for run in RUNS:
+            e, first, width = run
+            product = slots.tile([C, width], F32, name="product")
             nc.vector.tensor_tensor(
                 product[:],
-                tables[e][:].indirect(offsets[:, e * COLS : (e + 1) * COLS]),
-                gates[e][:],
+                tables[e][:].indirect(offsets[:, first // 16 : (first + width) // 16]),
+                gates[run][:],
                 MULT,
             )
-            rounded_e = slots.tile([C, K], BF16, name="rounded_e")
-            nc.vector.tensor_copy(rounded_e[:], product[:])
-            rounded.append(rounded_e)
+            rounded_run = slots.tile([C, width], BF16, name="rounded_run")
+            nc.vector.tensor_copy(rounded_run[:], product[:])
+            rounded[run] = rounded_run
 
-        def expand(e, b):
-            bank = banks.tile([P, K], F32, name="bank")
-            nc.tensor.matmul(bank[:], weights[e][:, b, :], rounded[e][:], start=True, stop=True)
-            return bank
-
-        for e in range(2):
+        for run in RUNS:
+            e, first, width = run
             for b in range(MB):
-                bank = expand(e, b)
-                single = singles.tile([P, K], F32, name="single")
-                nc.scalar.activation(single[:], bank[:], IDENTITY, bias=bias_cols[:, b : b + 1])
-                nc.sync.dma_start(out_groups[:, b, e * K : (e + 1) * K], single[:])
-
-        for b in range(MB):
-            bank2 = expand(2, b)
-            bank3 = expand(3, b)
-            double = doubles.tile([P, 2 * K], F32, name="double")
-            nc.scalar.activation(double[:, :K], bank2[:], IDENTITY, bias=bias_cols[:, b : b + 1])
-            nc.vector.tensor_scalar_add(double[:, K:], bank3[:], bias_cols[:, b : b + 1])
-            nc.sync.dma_start(out_groups[:, b, 2 * K :], double[:])
+                bank = banks.tile([P, width], F32, name="bank")
+                nc.tensor.matmul(bank[:], weights[e][:, b, :], rounded[run][:], start=True, stop=True)
+                ready = staged.tile([P, width], F32, name="ready")
+                if e >= 2 and b % 2 == 0:
+                    nc.vector.tensor_scalar_add(ready[:], bank[:], bias_cols[:, b : b + 1])
+                else:
+                    nc.scalar.activation(ready[:], bank[:], IDENTITY, bias=bias_cols[:, b : b + 1])
+                nc.sync.dma_start(out_groups[:, b, first : first + width], ready[:])

@@ -18,7 +18,7 @@ def tile_expertschoosemaskedexpand_kernel(tc, x, gate, w, bias, offs, out):
     with (
         tc.tile_pool(name="held", bufs=1) as held,
         tc.tile_pool(name="slots", bufs=len(RUNS)) as slots,
-        tc.tile_pool(name="staged", bufs=len(RUNS) * MB) as staged,
+        tc.tile_pool(name="staged", bufs=len(RUNS)) as staged,
         tc.psum_pool(name="banks", bufs=8) as banks,
     ):
         offsets = held.tile([P, N // 16], U16, name="offsets")
@@ -56,12 +56,12 @@ def tile_expertschoosemaskedexpand_kernel(tc, x, gate, w, bias, offs, out):
 
         for run in RUNS:
             e, first, width = run
+            ready = staged.tile([P, MB, width], F32, name="ready")
             for b in range(MB):
                 bank = banks.tile([P, width], F32, name="bank")
                 nc.tensor.matmul(bank[:], weights[e][:, b, :], rounded[run][:], start=True, stop=True)
-                ready = staged.tile([P, width], F32, name="ready")
                 if e >= 2 and b % 2 == 0:
-                    nc.vector.tensor_scalar_add(ready[:], bank[:], bias_cols[:, b : b + 1])
+                    nc.vector.tensor_scalar_add(ready[:, b, :], bank[:], bias_cols[:, b : b + 1])
                 else:
-                    nc.scalar.activation(ready[:], bank[:], IDENTITY, bias=bias_cols[:, b : b + 1])
-                nc.sync.dma_start(out_groups[:, b, first : first + width], ready[:])
+                    nc.scalar.activation(ready[:, b, :], bank[:], IDENTITY, bias=bias_cols[:, b : b + 1])
+            nc.sync.dma_start(out_groups[:, :, first : first + width], ready[:])

@@ -7,7 +7,7 @@ F32, BF16, U16 = mybir.dt.float32, mybir.dt.bfloat16, mybir.dt.uint16
 MULT = mybir.AluOpType.mult
 IDENTITY = mybir.ActivationFunctionType.Identity
 
-RUNS = [(0, 0, K // 2), (0, K // 2, K // 2)] + [(e, e * K, K) for e in range(1, E)]
+RUNS = [(0, 0, K // 2, MB), (0, K // 2, K // 2, MB), (1, K, K, 1), (2, 2 * K, K, 1), (3, 3 * K, K, 2)]
 
 FLOPS = 2 * C * M * N
 
@@ -18,7 +18,7 @@ def tile_expertschoosemaskedexpand_kernel(tc, x, gate, w, bias, offs, out):
     with (
         tc.tile_pool(name="held", bufs=1) as held,
         tc.tile_pool(name="slots", bufs=len(RUNS)) as slots,
-        tc.tile_pool(name="staged", bufs=len(RUNS)) as staged,
+        tc.tile_pool(name="staged", bufs=sum(MB // run[3] for run in RUNS)) as staged,
         tc.psum_pool(name="banks", bufs=8) as banks,
     ):
         offsets = held.tile([P, N // 16], U16, name="offsets")
@@ -42,7 +42,7 @@ def tile_expertschoosemaskedexpand_kernel(tc, x, gate, w, bias, offs, out):
 
         rounded = {}
         for run in RUNS:
-            e, first, width = run
+            e, first, width = run[:3]
             product = slots.tile([C, width], F32, name="product")
             nc.vector.tensor_tensor(
                 product[:],
@@ -55,13 +55,16 @@ def tile_expertschoosemaskedexpand_kernel(tc, x, gate, w, bias, offs, out):
             rounded[run] = rounded_run
 
         for run in RUNS:
-            e, first, width = run
-            ready = staged.tile([P, MB, width], F32, name="ready")
-            for b in range(MB):
-                bank = banks.tile([P, width], F32, name="bank")
-                nc.tensor.matmul(bank[:], weights[e][:, b, :], rounded[run][:], start=True, stop=True)
-                if e >= 2 and b % 2 == 0:
-                    nc.vector.tensor_scalar_add(ready[:, b, :], bank[:], bias_cols[:, b : b + 1])
-                else:
-                    nc.scalar.activation(ready[:, b, :], bank[:], IDENTITY, bias=bias_cols[:, b : b + 1])
-            nc.sync.dma_start(out_groups[:, :, first : first + width], ready[:])
+            e, first, width, per_store = run
+            for b0 in range(0, MB, per_store):
+                ready = staged.tile([P, per_store, width], F32, name="ready")
+                for b in range(b0, b0 + per_store):
+                    bank = banks.tile([P, width], F32, name="bank")
+                    nc.tensor.matmul(bank[:], weights[e][:, b, :], rounded[run][:], start=True, stop=True)
+                    if e >= 2 and b >= MB // 2:
+                        nc.vector.tensor_scalar_add(ready[:, b - b0, :], bank[:], bias_cols[:, b : b + 1])
+                    else:
+                        nc.scalar.activation(
+                            ready[:, b - b0, :], bank[:], IDENTITY, bias=bias_cols[:, b : b + 1]
+                        )
+                nc.sync.dma_start(out_groups[:, b0 : b0 + per_store, first : first + width], ready[:])

@@ -21,24 +21,38 @@ def tile_expertschoosemaskedexpand_kernel(tc, x, gate, w, bias, offs, out):
         tc.tile_pool(name="staged", bufs=sum(MB // run[3] for run in RUNS)) as staged,
         tc.psum_pool(name="banks", bufs=8) as banks,
     ):
+        def load(shape, dtype, name, source):
+            tile = held.tile(shape, dtype, name=name)
+            nc.sync.dma_start(tile[:], source)
+            return tile
+
+        def load_table(e):
+            return load([C, S], F32, f"table{e}", x[e])
+
+        def load_gate(first, width):
+            return load([C, width], F32, f"gate{first}", gate[:, first : first + width])
+
+        def load_weights(e, count):
+            return load([C, count, M], BF16, f"weight{e}", w[e : e + count].rearrange("e c m -> c e m"))
+
         offsets = held.tile([P, N // 16], U16, name="offsets")
         nc.sync.dma_start(offsets[:], offs)
-        bias_cols = held.tile([P, MB], F32, name="bias_cols")
-        tables, weights, gates = {}, {}, {}
-        for e in range(E):
-            table = held.tile([C, S], F32, name=f"table{e}")
-            nc.sync.dma_start(table[:], x[e])
-            tables[e] = table
-            for run in RUNS:
-                if run[0] == e:
-                    gate_run = held.tile([C, run[2]], F32, name=f"gate{run[1]}")
-                    nc.sync.dma_start(gate_run[:], gate[:, run[1] : run[1] + run[2]])
-                    gates[run] = gate_run
-            weight = held.tile([C, M], BF16, name=f"weight{e}")
-            nc.sync.dma_start(weight[:], w[e])
-            weights[e] = weight[:].rearrange("c (p b) -> c b p", b=MB)
-            if e == 0:
-                nc.sync.dma_start(bias_cols[:], bias.rearrange("(p b) o -> p (b o)", b=MB))
+        tables, gates = {}, {}
+        tables[0] = load_table(0)
+        gates[RUNS[0]] = load_gate(0, K // 2)[:]
+        gates[RUNS[1]] = load_gate(K // 2, K // 2)[:]
+        weight0 = load_weights(0, 1)
+        bias_cols = load([P, MB], F32, "bias_cols", bias.rearrange("(p b) o -> p (b o)", b=MB))
+        tables[1] = load_table(1)
+        gates[RUNS[2]] = load_gate(K, K)[:]
+        tables[2] = load_table(2)
+        gate23 = load_gate(2 * K, 2 * K)
+        gates[RUNS[3]] = gate23[:, :K]
+        gates[RUNS[4]] = gate23[:, K:]
+        weight123 = load_weights(1, E - 1)
+        tables[3] = load_table(3)
+        weights = [weight0[:, 0, :]] + [weight123[:, e - 1, :] for e in range(1, E)]
+        weights = [weight.rearrange("c (p b) -> c b p", b=MB) for weight in weights]
 
         rounded = {}
         for run in RUNS:
@@ -47,7 +61,7 @@ def tile_expertschoosemaskedexpand_kernel(tc, x, gate, w, bias, offs, out):
             nc.vector.tensor_tensor(
                 product[:],
                 tables[e][:].indirect(offsets[:, first // 16 : (first + width) // 16]),
-                gates[run][:],
+                gates[run],
                 MULT,
             )
             rounded_run = slots.tile([C, width], BF16, name="rounded_run")

@@ -7,7 +7,7 @@ F32, BF16, U16 = mybir.dt.float32, mybir.dt.bfloat16, mybir.dt.uint16
 MULT = mybir.AluOpType.mult
 IDENTITY = mybir.ActivationFunctionType.Identity
 
-RUNS = [(0, 0, K // 2, MB), (0, K // 2, K // 2, MB), (1, K, K, 1), (2, 2 * K, K, 1), (3, 3 * K, K, 2)]
+RUNS = [(0, 0, K // 2), (0, K // 2, K // 2)] + [(e, e * K, K) for e in range(1, E)]
 
 FLOPS = 2 * C * M * N
 
@@ -18,7 +18,7 @@ def tile_expertschoosemaskedexpand_kernel(tc, x, gate, w, bias, offs, out):
     with (
         tc.tile_pool(name="held", bufs=1) as held,
         tc.tile_pool(name="slots", bufs=len(RUNS)) as slots,
-        tc.tile_pool(name="staged", bufs=sum(MB // run[3] for run in RUNS)) as staged,
+        tc.tile_pool(name="staged", bufs=len(RUNS) * MB) as staged,
         tc.psum_pool(name="banks", bufs=8) as banks,
     ):
         def load(shape, dtype, name, source):
@@ -56,7 +56,7 @@ def tile_expertschoosemaskedexpand_kernel(tc, x, gate, w, bias, offs, out):
 
         rounded = {}
         for run in RUNS:
-            e, first, width = run[:3]
+            e, first, width = run
             product = slots.tile([C, width], F32, name="product")
             nc.vector.tensor_tensor(
                 product[:],
@@ -69,16 +69,13 @@ def tile_expertschoosemaskedexpand_kernel(tc, x, gate, w, bias, offs, out):
             rounded[run] = rounded_run
 
         for run in RUNS:
-            e, first, width, per_store = run
-            for b0 in range(0, MB, per_store):
-                ready = staged.tile([P, per_store, width], F32, name="ready")
-                for b in range(b0, b0 + per_store):
-                    bank = banks.tile([P, width], F32, name="bank")
-                    nc.tensor.matmul(bank[:], weights[e][:, b, :], rounded[run][:], start=True, stop=True)
-                    if e >= 2 and b >= MB // 2:
-                        nc.vector.tensor_scalar_add(ready[:, b - b0, :], bank[:], bias_cols[:, b : b + 1])
-                    else:
-                        nc.scalar.activation(
-                            ready[:, b - b0, :], bank[:], IDENTITY, bias=bias_cols[:, b : b + 1]
-                        )
-                nc.sync.dma_start(out_groups[:, b0 : b0 + per_store, first : first + width], ready[:])
+            e, first, width = run
+            for b in range(MB):
+                bank = banks.tile([P, width], F32, name="bank")
+                nc.tensor.matmul(bank[:], weights[e][:, b, :], rounded[run][:], start=True, stop=True)
+                ready = staged.tile([P, width], F32, name="ready")
+                if e >= 2 and b % 2 == 0:
+                    nc.vector.tensor_scalar_add(ready[:], bank[:], bias_cols[:, b : b + 1])
+                else:
+                    nc.scalar.activation(ready[:], bank[:], IDENTITY, bias=bias_cols[:, b : b + 1])
+                nc.sync.dma_start(out_groups[:, b, first : first + width], ready[:])

@@ -9,6 +9,8 @@ IDENTITY = mybir.ActivationFunctionType.Identity
 
 RUNS = [(0, 0, K // 2), (0, K // 2, K // 2)] + [(e, e * K, K) for e in range(1, E)]
 
+LINE = 512
+
 FLOPS = 2 * C * M * N
 
 
@@ -22,7 +24,7 @@ def tile_expertschoosemaskedexpand_kernel(tc, x, gate, w, bias, offs, out):
         tc.psum_pool(name="banks", bufs=8) as banks,
     ):
         def load(shape, dtype, name, source):
-            tile = held.tile(shape, dtype, name=name)
+            tile = held.tile(shape, dtype, name=name, align_bytes=LINE)
             nc.sync.dma_start(tile[:], source)
             return tile
 
@@ -35,7 +37,7 @@ def tile_expertschoosemaskedexpand_kernel(tc, x, gate, w, bias, offs, out):
         def load_weights(e, count):
             return load([C, count, M], BF16, f"weight{e}", w[e : e + count].rearrange("e c m -> c e m"))
 
-        offsets = held.tile([P, N // 16], U16, name="offsets")
+        offsets = held.tile([P, N // 16], U16, name="offsets", align_bytes=LINE)
         nc.sync.dma_start(offsets[:], offs)
         tables, gates = {}, {}
         tables[0] = load_table(0)
@@ -73,7 +75,7 @@ def tile_expertschoosemaskedexpand_kernel(tc, x, gate, w, bias, offs, out):
             for b in range(MB):
                 bank = banks.tile([P, width], F32, name="bank")
                 nc.tensor.matmul(bank[:], weights[e][:, b, :], rounded[run][:], start=True, stop=True)
-                ready = staged.tile([P, width], F32, name="ready")
+                ready = staged.tile([P, width], F32, name="ready", align_bytes=LINE)
                 if e >= 2 and b % 2 == 0:
                     nc.vector.tensor_scalar_add(ready[:], bank[:], bias_cols[:, b : b + 1])
                 else:

@@ -9,7 +9,7 @@ IDENTITY = mybir.ActivationFunctionType.Identity
 
 RUNS = [(0, 0, K // 2), (0, K // 2, K // 2)] + [(e, e * K, K) for e in range(1, E)]
 
-LINE = 512
+LINE = 4 * K
 
 FLOPS = 2 * C * M * N
 
@@ -59,14 +59,14 @@ def tile_expertschoosemaskedexpand_kernel(tc, x, gate, w, bias, offs, out):
         rounded = {}
         for run in RUNS:
             e, first, width = run
-            product = slots.tile([C, width], F32, name="product")
+            product = slots.tile([C, width], F32, name="product", align_bytes=LINE)
             nc.vector.tensor_tensor(
                 product[:],
                 tables[e][:].indirect(offsets[:, first // 16 : (first + width) // 16]),
                 gates[run],
                 MULT,
             )
-            rounded_run = slots.tile([C, width], BF16, name="rounded_run")
+            rounded_run = slots.tile([C, width], BF16, name="rounded_run", align_bytes=LINE)
             nc.vector.tensor_copy(rounded_run[:], product[:])
             rounded[run] = rounded_run
 

import concourse.mybir as mybir

E, C, S, K, M, N = 4, 128, 512, 512, 512, 2048
P = 128
MB = M // P
F32, BF16, U16 = mybir.dt.float32, mybir.dt.bfloat16, mybir.dt.uint16
MULT = mybir.AluOpType.mult
IDENTITY = mybir.ActivationFunctionType.Identity

RUNS = [(0, 0, K // 2), (0, K // 2, K // 2)] + [(e, e * K, K) for e in range(1, E)]

LINE = 4 * K

FLOPS = 2 * C * M * N


def tile_expertschoosemaskedexpand_kernel(tc, x, gate, w, bias, offs, out):
    nc = tc.nc
    out_groups = out.rearrange("(p b) n -> p b n", b=MB)
    with (
        tc.tile_pool(name="held", bufs=1) as held,
        tc.tile_pool(name="slots", bufs=len(RUNS)) as slots,
        tc.tile_pool(name="staged", bufs=len(RUNS) * MB) as staged,
        tc.psum_pool(name="banks", bufs=8) as banks,
    ):
        def load(shape, dtype, name, source):
            tile = held.tile(shape, dtype, name=name, align_bytes=LINE)
            nc.sync.dma_start(tile[:], source)
            return tile

        def load_table(e):
            return load([C, S], F32, f"table{e}", x[e])

        def load_gate(first, width):
            return load([C, width], F32, f"gate{first}", gate[:, first : first + width])

        def load_weights(e, count):
            return load([C, count, M], BF16, f"weight{e}", w[e : e + count].rearrange("e c m -> c e m"))

        offsets = held.tile([P, N // 16], U16, name="offsets", align_bytes=LINE)
        nc.sync.dma_start(offsets[:], offs)
        tables, gates = {}, {}
        tables[0] = load_table(0)
        gates[RUNS[0]] = load_gate(0, K // 2)[:]
        gates[RUNS[1]] = load_gate(K // 2, K // 2)[:]
        weight0 = load_weights(0, 1)
        bias_cols = load([P, MB], F32, "bias_cols", bias.rearrange("(p b) o -> p (b o)", b=MB))
        tables[1] = load_table(1)
        gates[RUNS[2]] = load_gate(K, K)[:]
        tables[2] = load_table(2)
        gate23 = load_gate(2 * K, 2 * K)
        gates[RUNS[3]] = gate23[:, :K]
        gates[RUNS[4]] = gate23[:, K:]
        weight123 = load_weights(1, E - 1)
        tables[3] = load_table(3)
        weights = [weight0[:, 0, :]] + [weight123[:, e - 1, :] for e in range(1, E)]
        weights = [weight.rearrange("c (p b) -> c b p", b=MB) for weight in weights]

        rounded = {}
        for run in RUNS:
            e, first, width = run
            product = slots.tile([C, width], F32, name="product", align_bytes=LINE)
            nc.vector.tensor_tensor(
                product[:],
                tables[e][:].indirect(offsets[:, first // 16 : (first + width) // 16]),
                gates[run],
                MULT,
            )
            rounded_run = slots.tile([C, width], BF16, name="rounded_run", align_bytes=LINE)
            nc.vector.tensor_copy(rounded_run[:], product[:])
            rounded[run] = rounded_run

        for run in RUNS:
            e, first, width = run
            for b in range(MB):
                bank = banks.tile([P, width], F32, name="bank")
                nc.tensor.matmul(bank[:], weights[e][:, b, :], rounded[run][:], start=True, stop=True)
                ready = staged.tile([P, width], F32, name="ready", align_bytes=LINE)
                if e >= 2 and b % 2 == 0:
                    nc.vector.tensor_scalar_add(ready[:], bank[:], bias_cols[:, b : b + 1])
                else:
                    nc.scalar.activation(ready[:], bank[:], IDENTITY, bias=bias_cols[:, b : b + 1])
                nc.sync.dma_start(out_groups[:, b, first : first + width], ready[:])
